import numpy as np
import ml_dtypes


def mxq(x, axis, fmt="e4m3"):
    dtype, down = {"e4m3": (ml_dtypes.float8_e4m3fn, 7), "e5m2": (ml_dtypes.float8_e5m2, 14)}[fmt]
    v = np.moveaxis(np.asarray(x, np.float32).astype(ml_dtypes.bfloat16).astype(np.float64), axis, -1)
    blocks = v.reshape(v.shape[:-1] + (-1, 32))
    amax = np.abs(blocks).max(-1, keepdims=True)
    byte = np.maximum(np.where(amax > 0, np.frexp(amax)[1] - 1 + 127, 0) - down, 1)
    scale = np.exp2(byte - 127.0)
    codes = (blocks / scale).astype(np.float32).astype(dtype).astype(np.float64)
    return np.moveaxis((codes * scale).reshape(v.shape), -1, axis)


WIDE = False


def mx_kscale(k):
    if not WIDE:
        return np.ones(k)
    levels = np.array([10, -10, 5, -5, 0])
    if k % 512:
        return np.exp2(np.random.permutation(np.resize(levels, k // 32))).repeat(32)
    a = np.empty((k // 512, 16))
    for p in range(k // 512):
        a[p, :8] = np.random.permutation(np.resize(levels, 8))
        for g in range(8):
            far = levels[np.abs(levels - a[p, g]) >= 10]
            a[p, g + 8] = far[np.random.randint(len(far))]
    return np.exp2(a.ravel()).repeat(32)


BF16 = ml_dtypes.bfloat16


def bf(x):
    return np.asarray(x, np.float32).astype(BF16)


def f64(x):
    return np.asarray(x).astype(np.float64)


B, IN, H, G, GA, GB = 4096, 512, 512, 6, 4, 2
EPS = 1e-5


def layer_norm(v, g, b):
    mu = v.mean(-1, keepdims=True)
    var = np.square(v - mu).mean(-1, keepdims=True)
    return (v - mu) / np.sqrt(var + EPS) * g + b


def sigmoid(v):
    return 1.0 / (1.0 + np.exp(-v))


def setup_inputs():
    s, t = mx_kscale(IN), mx_kscale(H)
    return {"x": bf(np.random.standard_normal((B, IN)) * s),
            "h": bf(np.random.standard_normal((B, H)) * t),
            "W_r": bf(np.random.standard_normal((H, H)) / np.sqrt(H) / t),
            "U_r": bf(np.random.standard_normal((H, IN)) / np.sqrt(IN) / s),
            "W_c": bf(np.random.standard_normal((H, H)) / np.sqrt(H) / t),
            "U_c": bf(np.random.standard_normal((H, IN)) / np.sqrt(IN) / s),
            "ln_gamma": bf(1.0 + 0.1 * np.random.standard_normal((GA, H))),
            "ln_beta": bf(0.2 * np.random.standard_normal((GA, H)))}


def reference(x, h, W_r, U_r, W_c, U_c, ln_gamma, ln_beta):
    g_rh, g_rx, g_ch, g_cx = f64(ln_gamma)
    b_rh, b_rx, b_ch, b_cx = f64(ln_beta)
    hf = f64(h)
    xq = mxq(f64(x), 1, "e4m3")
    r = sigmoid(layer_norm(mxq(hf, 1, "e4m3") @ mxq(f64(W_r), 1, "e4m3").T, g_rh, b_rh)
                + layer_norm(xq @ mxq(f64(U_r), 1, "e4m3").T, g_rx, b_rx))
    return np.tanh(layer_norm(mxq(hf * r, 1, "e4m3") @ mxq(f64(W_c), 1, "e4m3").T, g_ch, b_ch)
                   + layer_norm(xq @ mxq(f64(U_c), 1, "e4m3").T, g_cx, b_cx))

@@ -1,0 +1,387 @@
+from contextlib import ExitStack
+
+import concourse.mybir as mybir
+from concourse.masks import make_identity
+
+F32 = mybir.dt.float32
+BF16 = mybir.dt.bfloat16
+U32 = mybir.dt.uint32
+U8 = mybir.dt.uint8
+FP8X4 = mybir.dt.float8_e4m3fn_x4
+ACT = mybir.ActivationFunctionType
+ALU = mybir.AluOpType
+
+P = 128
+ROWS = 4096
+D = 512
+ST = 512
+NST = ROWS // ST
+NJ = ST // P
+NT = D // P
+EPS = 1e-5
+FLOPS = 4 * 2 * ROWS * D * D
+
+CHAIN = 2
+NORM_LAG = 4
+GAIN_LAG = NORM_LAG + 5
+ACT_LAG = GAIN_LAG + 4
+MUL_LAG = ACT_LAG + 4
+QUANT_LAG = MUL_LAG + 2
+STAGE_GAP = 5
+INPUT_LEAD = 5
+LOAD_LEAD = 3
+LATE_WEIGHTS = 10
+GAIN_TABLES = 5
+SCALAR_COPIES_UPTO = 2
+VECTOR_NORMS_LAST_UNITS = 4
+G_ROWS = 64
+
+
+def unit_order():
+    order = [(s, 1) for s in range(STAGE_GAP)]
+    for s in range(NST - STAGE_GAP):
+        order += [(s, 2), (s + STAGE_GAP, 1)]
+    return order + [(s, 2) for s in range(NST - STAGE_GAP, NST)]
+
+
+def tile_layernormgrucell_pa_t_kernel(tc, x, h, W_r, U_r, W_c, U_c, ln_gamma, ln_beta, out):
+    nc = tc.nc
+    x_v = x.rearrange("(s j p) k -> p s j k", s=NST, j=NJ)
+    h_v = h.rearrange("(s j p) k -> p s j k", s=NST, j=NJ)
+    out_v = out.rearrange("(s j p) f -> p s j f", s=NST, j=NJ)
+    units = unit_order()
+    slots = NJ * len(units)
+    first_slot = {s: NJ * units.index((s, 1)) for s in range(NST)}
+
+    with ExitStack() as ctx:
+        ctx.enter_context(tc.manual_schedule())
+        const = ctx.enter_context(tc.tile_pool(name="const", bufs=1))
+        wpool = ctx.enter_context(tc.tile_pool(name="wpool", bufs=2))
+        io = ctx.enter_context(tc.tile_pool(name="io", bufs=2))
+        words = ctx.enter_context(tc.tile_pool(name="words", bufs=2))
+        codes = ctx.enter_context(tc.tile_pool(name="codes", bufs=4))
+        normed = ctx.enter_context(tc.tile_pool(name="normed", bufs=3))
+        sums = ctx.enter_context(tc.tile_pool(name="sums", bufs=4))
+        outs = ctx.enter_context(tc.tile_pool(name="outs", bufs=4))
+        small = ctx.enter_context(tc.tile_pool(name="small", bufs=6))
+        mx_banks = ctx.enter_context(tc.psum_pool(name="mx_banks", bufs=4))
+        tr_banks = ctx.enter_context(tc.psum_pool(name="tr_banks", bufs=4))
+
+        ident = const.tile([P, P], F32, name="ident")
+        make_identity(nc, ident[:])
+        minus_half = const.tile([P, 2 * CHAIN], F32, name="minus_half")
+        nc.gpsimd.memset(minus_half[:], -0.5)
+        warm = const.tile([P, 1], F32, name="warm")
+        nc.vector.memset(warm[:], 0.0)
+        nc.scalar.activation(out=warm[:], in_=warm[:], func=ACT.Sigmoid)
+
+        def words_to_bank(pool, src, first):
+            bank = pool.tile([P, 2, 2 * P], F32, tag="bank")
+            for i in range(2):
+                src32 = src[:, first + i, :].bitcast(F32).rearrange("p (w u) -> p u w", u=2)
+                for u in range(2):
+                    nc.tensor.transpose(bank[:, u, i * P:(i + 1) * P], src32[:, u, :], ident[:])
+            return bank
+
+        def bank_to_words(dst, half, bank, on_scalar):
+            dst32 = dst[:].bitcast(F32).rearrange("p (n u) -> p n u", u=2)[:, half * 2 * P:(half + 1) * 2 * P, :]
+            if on_scalar:
+                nc.scalar.copy(out=dst32, in_=bank[:].rearrange("p u n -> p n u"))
+            else:
+                nc.vector.tensor_copy(out=dst32, in_=bank[:].rearrange("p u n -> p n u"))
+
+        def quantise(code_words, scales, src):
+            nc.vector.quantize_mx(out=code_words.bitcast(FP8X4), scales=scales, in_=src)
+
+        w_raw = {}
+        w_words = {}
+        w_codes = [const.tile([P, D], U32, name="w_codes%d" % i, align_bytes=64) for i in range(4)]
+        w_scales = [const.tile([P, D], U8, name="w_scales%d" % i, align_bytes=64) for i in range(4)]
+
+        def load_weight(i, w):
+            raw = wpool.tile([P, NT, D], BF16, tag="raw", bufs=4)
+            if i < 2:
+                nc.sync.dma_start(out=raw[:], in_=w.rearrange("(p t) k -> p t k", t=NT))
+            else:
+                nc.sync.dma_start(out=raw[:], in_=w.rearrange("(t p) k -> p t k", p=P))
+            w_raw[i] = raw
+
+        def weight_words(i, half, pool):
+            if half == 0:
+                grouped = wpool.tile([P, 4 * D], BF16, tag="grouped", align_bytes=64)
+                w_words[i] = grouped
+            bank_to_words(w_words[i], half, words_to_bank(pool, w_raw[i], 2 * half), half == 1)
+
+        def quantise_weight(i):
+            quantise(w_codes[i][:], w_scales[i][:], w_words[i][:])
+
+        rows_in = {}
+        h_words = {}
+        x_words = {}
+        in_banks = {}
+        h_codes = {}
+        x_codes = const.tile([P, NST, ST], U32, name="x_codes", align_bytes=64)
+        x_scales = const.tile([P, NST, ST], U8, name="x_scales", align_bytes=64)
+
+        def load_rows(s):
+            h_sb = io.tile([P, NJ, D], BF16, tag="h_sb")
+            nc.sync.dma_start(out=h_sb[:], in_=h_v[:, s])
+            x_sb = io.tile([P, NJ, D], BF16, tag="x_sb")
+            nc.sync.dma_start(out=x_sb[:], in_=x_v[:, s])
+            rows_in[s] = (h_sb, x_sb)
+
+        def input_transposes(s, piece, pool):
+            if piece == 0:
+                h_w = words.tile([P, 4 * ST], BF16, tag="h_w", bufs=6, align_bytes=64)
+                x_w = words.tile([P, 4 * ST], BF16, tag="x_w", align_bytes=64)
+                h_words[s] = h_w
+                x_words[s] = x_w
+            in_banks[(s, piece)] = words_to_bank(pool, rows_in[s][piece // 2], 2 * (piece % 2))
+
+        def input_copy(s, piece):
+            on_scalar = piece % 2 == 1 if s == 0 else s <= SCALAR_COPIES_UPTO
+            bank_to_words(h_words[s] if piece < 2 else x_words[s], piece % 2, in_banks[(s, piece)], on_scalar)
+
+        def quantise_h(s):
+            c_w = codes.tile([P, ST], U32, tag="h_codes", align_bytes=64)
+            c_s = codes.tile([P, ST], U8, tag="h_scales", align_bytes=64)
+            quantise(c_w[:], c_s[:], h_words[s][:])
+            h_codes[s] = (c_w, c_s)
+
+        def quantise_x(s):
+            quantise(x_codes[:, s, :], x_scales[:, s, :], x_words[s][:])
+
+        def gain_tables():
+            strided = params32[:].rearrange("p (q t) -> p t q", t=NT)
+            tables = []
+            for stage in (1, 2):
+                bank = tr_banks.tile([P, NT, P], F32, tag="bank")
+                for t in range(NT):
+                    chunk = strided[:, t, :] if stage == 1 else params32[:, t * P:(t + 1) * P]
+                    nc.tensor.transpose(bank[:, t, :], chunk, ident[:])
+                table = const.tile([P, 8, NT], F32, name="table%d" % stage)
+                nc.vector.tensor_copy(out=table[:], in_=bank[:, :, 0:8].rearrange("p c i -> p i c"))
+                bias = const.tile([P, NT], F32, name="bias%d" % stage)
+                nc.vector.tensor_tensor(out=bias[:], in0=table[:, 2 + 2 * stage, :], in1=table[:, 3 + 2 * stage, :],
+                                        op=ALU.add)
+                tables.append((table, bias))
+            return tables
+
+        hr_codes = {}
+        stat_banks = {}
+        stat_parts = {}
+        moments = {}
+
+        def products(unit, j):
+            s, stage = unit
+            cols = slice(j * P, (j + 1) * P)
+            a_w, a_s = h_codes[s] if stage == 1 else hr_codes[s]
+            pair = []
+            for lhs_w, lhs_s, i in ((a_w[:, cols], a_s[:, cols], 2 * stage - 2),
+                                    (x_codes[:, s, cols], x_scales[:, s, cols], 2 * stage - 1)):
+                bank = mx_banks.tile([P, D], F32, tag="bank")
+                nc.tensor.matmul_mx(out=bank[:], lhsT=lhs_w.bitcast(FP8X4), lhsT_scale=lhs_s,
+                                    rhs=w_codes[i][:].bitcast(FP8X4), rhs_scale=w_scales[i][:], start=True, stop=True)
+                pair.append(bank)
+            return pair
+
+        def products_for_statistics(unit, j):
+            stat_banks[(unit, j)] = products(unit, j)
+
+        def statistics(unit, j):
+            parts = small.tile([P, 2, 6], F32, tag="parts")
+            for side in range(2):
+                nc.vector.bn_stats(out=parts[:, side, :], in_=stat_banks[(unit, j)][side][:])
+            stat_parts[(unit, j)] = parts
+
+        def finish_statistics(unit, j):
+            k = 2 * (j % CHAIN)
+            if k == 0:
+                mean_var = small.tile([P, 2 * CHAIN, 2], F32, tag="mean_var")
+                moments[(unit, j // CHAIN)] = [mean_var]
+            mean_var = moments[(unit, j // CHAIN)][0]
+            for side in range(2):
+                nc.vector.bn_aggr(out=mean_var[:, k + side, :], in_=stat_parts[(unit, j)][:, side, :])
+            if j % CHAIN == CHAIN - 1:
+                var_eps = small.tile([P, 2 * CHAIN], F32, tag="var_eps")
+                nc.gpsimd.tensor_scalar(out=var_eps[:], in0=mean_var[:, :, 1], scalar1=1.0, scalar2=EPS,
+                                        op0=ALU.mult, op1=ALU.add)
+                rstd = small.tile([P, 2 * CHAIN], F32, tag="rstd")
+                nc.gpsimd.tensor_tensor(out=rstd[:], in0=var_eps[:], in1=minus_half[:], op=ALU.pow)
+                mean_rstd = small.tile([P, 2 * CHAIN], F32, tag="mean_rstd")
+                nc.gpsimd.tensor_tensor(out=mean_rstd[:], in0=mean_var[:, :, 0], in1=rstd[:], op=ALU.mult)
+                shift = small.tile([P, 2 * CHAIN], F32, tag="shift")
+                nc.gpsimd.tensor_scalar(out=shift[:], in0=mean_rstd[:], scalar1=-1.0, scalar2=0.0,
+                                        op0=ALU.mult, op1=ALU.add)
+                moments[(unit, j // CHAIN)] += [rstd, shift]
+
+        norm_banks = {}
+        normal = {}
+
+        def products_to_normalise(unit, j):
+            norm_banks[(unit, j)] = products(unit, j)
+
+        def on_vector(unit, j, side):
+            return side == 1 and j % 2 == 1 and units.index(unit) >= len(units) - VECTOR_NORMS_LAST_UNITS
+
+        def normalise(unit, j, vector_turn):
+            if j == 0 and not vector_turn:
+                n_a = normed.tile([P, NJ, D], F32, tag="n_a")
+                n_b = normed.tile([P, NJ, D], F32, tag="n_b")
+                normal[unit] = (n_a, n_b)
+            mean_var, rstd, shift = moments[(unit, j // CHAIN)]
+            for side in range(2):
+                k = 2 * (j % CHAIN) + side
+                if on_vector(unit, j, side) != vector_turn:
+                    continue
+                if vector_turn:
+                    nc.vector.tensor_scalar(out=normal[unit][side][:, j, :], in0=norm_banks[(unit, j)][side][:],
+                                            scalar1=mean_var[:, k, 0:1], scalar2=rstd[:, k:k + 1],
+                                            op0=ALU.subtract, op1=ALU.mult)
+                else:
+                    nc.scalar.activation(out=normal[unit][side][:, j, :], in_=norm_banks[(unit, j)][side][:],
+                                         func=ACT.Identity, bias=shift[:, k:k + 1], scale=rstd[:, k:k + 1])
+
+        def normalise_on_scalar(unit, j):
+            normalise(unit, j, False)
+
+        def normalise_on_vector(unit, j):
+            normalise(unit, j, True)
+
+        feat_banks = {}
+        summed = {}
+
+        def to_features(unit, t, side):
+            bank = tr_banks.tile([P, ST], F32, tag="bank")
+            for j in range(NJ):
+                nc.tensor.transpose(bank[:, j * P:(j + 1) * P], normal[unit][side][:, j, t * P:(t + 1) * P], ident[:])
+            feat_banks[(unit, t, side)] = bank
+
+        def first_gain(unit, t):
+            if t == 0:
+                z = sums.tile([P, NT, ST], F32, tag="z")
+                summed[unit] = z
+            table, bias = tables[unit[1] - 1]
+            nc.scalar.activation(out=summed[unit][:, t, :], in_=feat_banks[(unit, t, 0)][:], func=ACT.Identity,
+                                 bias=bias[:, t:t + 1], scale=table[:, 2 * unit[1] - 2, t:t + 1])
+
+        def second_gain(unit, t):
+            table, bias = tables[unit[1] - 1]
+            z = summed[unit]
+            nc.vector.scalar_tensor_tensor(out=z[:, t, :], in0=feat_banks[(unit, t, 1)][:],
+                                           scalar=table[:, 2 * unit[1] - 1, t:t + 1], in1=z[:, t, :],
+                                           op0=ALU.mult, op1=ALU.add)
+
+        row_banks = {}
+
+        def to_rows(unit, i):
+            if unit[1] == 2:
+                bank = tr_banks.tile([P, D], F32, tag="bank")
+                for t in range(NT):
+                    nc.tensor.transpose(bank[:, t * P:(t + 1) * P], summed[unit][:, t, i * P:(i + 1) * P], ident[:])
+                row_banks[(unit, i)] = bank
+
+        def activate(unit, i):
+            if unit[1] == 1:
+                nc.scalar.activation(out=summed[unit][:, i, :], in_=summed[unit][:, i, :], func=ACT.Sigmoid)
+            else:
+                c_sb = outs.tile([P, D], F32, tag="c_sb")
+                nc.scalar.activation(out=c_sb[:], in_=row_banks[(unit, i)][:], func=ACT.Tanh)
+                nc.sync.dma_start(out=out_v[:, unit[0], i, :], in_=c_sb[:])
+
+        hr_words = {}
+
+        def multiply(unit, i):
+            s, stage = unit
+            if stage == 2:
+                return
+            if i == 0:
+                hr_w = words.tile([P, 4 * ST], BF16, tag="hr_w", align_bytes=64)
+                hr_words[s] = hr_w
+            for engine, lo, hi in ((nc.gpsimd, 0, G_ROWS), (nc.vector, G_ROWS, P)):
+                rows = slice(i * P + lo, i * P + hi)
+                engine.tensor_tensor(out=hr_words[s][:].rearrange("p (r t) -> p r t", t=4)[:, rows, :],
+                                     in0=summed[unit][:, :, rows].rearrange("p t r -> p r t"),
+                                     in1=h_words[s][:].rearrange("p (r t) -> p r t", t=4)[:, rows, :], op=ALU.mult)
+
+        def quantise_hr(unit, i):
+            s, stage = unit
+            if stage == 2:
+                return
+            if i == 0:
+                c_w = codes.tile([P, ST], U32, tag="hr_codes", bufs=5, align_bytes=64)
+                c_s = codes.tile([P, ST], U8, tag="hr_scales", bufs=5, align_bytes=64)
+                hr_codes[s] = (c_w, c_s)
+            c_w, c_s = hr_codes[s]
+            quantise(c_w[:, i * P:(i + 1) * P], c_s[:, i * P:(i + 1) * P], hr_words[s][:, i * 4 * P:(i + 1) * 4 * P])
+
+        def run(step, slot):
+            if 0 <= slot < slots:
+                step(units[slot // NJ], slot % NJ)
+
+        load_weight(0, W_r)
+        load_rows(0)
+        load_weight(1, U_r)
+        params = const.tile([P, D], BF16, name="params")
+        nc.vector.memset(params[:], 0.0)
+        nc.sync.dma_start(out=params[0:4, :], in_=ln_gamma)
+        nc.sync.dma_start(out=params[4:8, :], in_=ln_beta)
+        load_rows(1)
+        load_weight(2, W_c)
+        load_weight(3, U_c)
+
+        weight_words(0, 0, mx_banks)
+        weight_words(0, 1, mx_banks)
+        for piece in range(4):
+            input_transposes(0, piece, mx_banks if piece < 2 else tr_banks)
+            input_copy(0, piece)
+            if piece == 1:
+                quantise_weight(0)
+        quantise_h(0)
+        weight_words(1, 0, tr_banks)
+        weight_words(1, 1, tr_banks)
+        quantise_x(0)
+        quantise_weight(1)
+        params32 = const.tile([P, D], F32, name="params32")
+        nc.gpsimd.tensor_scalar(out=params32[:], in0=params[:], scalar1=1.0, scalar2=0.0, op0=ALU.mult, op1=ALU.add)
+        run(products_for_statistics, 0)
+
+        tables = []
+        for it in range(-1, slots + ACT_LAG + 1):
+            pieces = [(s, it - (first_slot[s] - INPUT_LEAD)) for s in range(1, NST)]
+            if 0 <= it - GAIN_LAG < slots:
+                to_features(units[(it - GAIN_LAG) // NJ], (it - GAIN_LAG) % NJ, 0)
+            run(to_rows, it - ACT_LAG)
+            for s, piece in pieces:
+                if 0 <= piece < 4:
+                    input_transposes(s, piece, tr_banks)
+            if 0 <= it - LATE_WEIGHTS < 4:
+                weight_words(2 + (it - LATE_WEIGHTS) // 2, (it - LATE_WEIGHTS) % 2, tr_banks)
+            if it == GAIN_TABLES:
+                tables.extend(gain_tables())
+            if 0 <= it - GAIN_LAG < slots:
+                to_features(units[(it - GAIN_LAG) // NJ], (it - GAIN_LAG) % NJ, 1)
+            run(products_to_normalise, it - NORM_LAG)
+            if it >= 1:
+                run(products_for_statistics, it)
+            run(first_gain, it - GAIN_LAG)
+            run(activate, it - ACT_LAG)
+            run(normalise_on_scalar, it - NORM_LAG)
+            for s, piece in pieces:
+                if 0 <= piece < 4:
+                    input_copy(s, piece)
+                if piece == 2:
+                    quantise_h(s)
+                if piece == 4:
+                    quantise_x(s)
+            if it - LATE_WEIGHTS in (2, 4):
+                quantise_weight(1 + (it - LATE_WEIGHTS) // 2)
+            run(quantise_hr, it - QUANT_LAG)
+            run(multiply, it - MUL_LAG)
+            run(finish_statistics, it - 1)
+            run(second_gain, it - GAIN_LAG)
+            run(normalise_on_vector, it - NORM_LAG)
+            run(statistics, it)
+            for s in range(2, NST):
+                if it == max(first_slot[s] - INPUT_LEAD - LOAD_LEAD, -1):
+                    load_rows(s)

@@ -14,56 +14,55 @@ ALU = mybir.AluOpType
 P = 128
 ROWS = 4096
 D = 512
-ST = 512
-NST = ROWS // ST
-NJ = ST // P
+PR = 256
+NP = ROWS // PR
+NJ = PR // P
 NT = D // P
 EPS = 1e-5
 FLOPS = 4 * 2 * ROWS * D * D
-
 CHAIN = 2
 NORM_LAG = 4
-GAIN_LAG = NORM_LAG + 5
-ACT_LAG = GAIN_LAG + 4
-MUL_LAG = ACT_LAG + 4
-QUANT_LAG = MUL_LAG + 2
-STAGE_GAP = 5
-INPUT_LEAD = 5
-LOAD_LEAD = 3
-LATE_WEIGHTS = 10
-GAIN_TABLES = 5
-SCALAR_COPIES_UPTO = 2
-VECTOR_NORMS_LAST_UNITS = 4
-G_ROWS = 64
+GAIN_LAG = NORM_LAG + 3
+GAIN2_LAG = GAIN_LAG + 0
+ACT_LAG = GAIN2_LAG + 2
+MUL_LAG = ACT_LAG + 1
+QUANT_LAG = MUL_LAG + 1
+STAGE_GAP = 7
+INPUT_LEAD = 4
+LOAD_LEAD = 4
+LATE_WEIGHTS = 2
+GAIN_TABLES = 4
+SCALAR_COPIES_UPTO = 8
+VLAST = 6
 
 
 def unit_order():
     order = [(s, 1) for s in range(STAGE_GAP)]
-    for s in range(NST - STAGE_GAP):
+    for s in range(NP - STAGE_GAP):
         order += [(s, 2), (s + STAGE_GAP, 1)]
-    return order + [(s, 2) for s in range(NST - STAGE_GAP, NST)]
+    return order + [(s, 2) for s in range(NP - STAGE_GAP, NP)]
 
 
 def tile_layernormgrucell_pa_t_kernel(tc, x, h, W_r, U_r, W_c, U_c, ln_gamma, ln_beta, out):
     nc = tc.nc
-    x_v = x.rearrange("(s j p) k -> p s j k", s=NST, j=NJ)
-    h_v = h.rearrange("(s j p) k -> p s j k", s=NST, j=NJ)
-    out_v = out.rearrange("(s j p) f -> p s j f", s=NST, j=NJ)
+    x_v = x.rearrange("(s j p) k -> p s j k", s=NP, j=NJ)
+    h_v = h.rearrange("(s j p) k -> p s j k", s=NP, j=NJ)
+    out_v = out.rearrange("(s j p) f -> p s j f", s=NP, j=NJ)
     units = unit_order()
     slots = NJ * len(units)
-    first_slot = {s: NJ * units.index((s, 1)) for s in range(NST)}
+    first_slot = {s: NJ * units.index((s, 1)) for s in range(NP)}
 
     with ExitStack() as ctx:
         ctx.enter_context(tc.manual_schedule())
         const = ctx.enter_context(tc.tile_pool(name="const", bufs=1))
         wpool = ctx.enter_context(tc.tile_pool(name="wpool", bufs=2))
-        io = ctx.enter_context(tc.tile_pool(name="io", bufs=2))
-        words = ctx.enter_context(tc.tile_pool(name="words", bufs=2))
+        io = ctx.enter_context(tc.tile_pool(name="io", bufs=4))
+        words = ctx.enter_context(tc.tile_pool(name="words", bufs=3))
         codes = ctx.enter_context(tc.tile_pool(name="codes", bufs=4))
-        normed = ctx.enter_context(tc.tile_pool(name="normed", bufs=3))
-        sums = ctx.enter_context(tc.tile_pool(name="sums", bufs=4))
+        normed = ctx.enter_context(tc.tile_pool(name="normed", bufs=4))
+        sums = ctx.enter_context(tc.tile_pool(name="sums", bufs=6))
         outs = ctx.enter_context(tc.tile_pool(name="outs", bufs=4))
-        small = ctx.enter_context(tc.tile_pool(name="small", bufs=6))
+        small = ctx.enter_context(tc.tile_pool(name="small", bufs=8))
         mx_banks = ctx.enter_context(tc.psum_pool(name="mx_banks", bufs=4))
         tr_banks = ctx.enter_context(tc.psum_pool(name="tr_banks", bufs=4))
 
@@ -120,8 +119,8 @@ def tile_layernormgrucell_pa_t_kernel(tc, x, h, W_r, U_r, W_c, U_c, ln_gamma, ln
         x_words = {}
         in_banks = {}
         h_codes = {}
-        x_codes = const.tile([P, NST, ST], U32, name="x_codes", align_bytes=64)
-        x_scales = const.tile([P, NST, ST], U8, name="x_scales", align_bytes=64)
+        x_codes = const.tile([P, NP, PR], U32, name="x_codes", align_bytes=64)
+        x_scales = const.tile([P, NP, PR], U8, name="x_scales", align_bytes=64)
 
         def load_rows(s):
             h_sb = io.tile([P, NJ, D], BF16, tag="h_sb")
@@ -132,19 +131,19 @@ def tile_layernormgrucell_pa_t_kernel(tc, x, h, W_r, U_r, W_c, U_c, ln_gamma, ln
 
         def input_transposes(s, piece, pool):
             if piece == 0:
-                h_w = words.tile([P, 4 * ST], BF16, tag="h_w", bufs=6, align_bytes=64)
-                x_w = words.tile([P, 4 * ST], BF16, tag="x_w", align_bytes=64)
+                h_w = words.tile([P, 4 * PR], BF16, tag="h_w", bufs=10, align_bytes=64)
+                x_w = words.tile([P, 4 * PR], BF16, tag="x_w", align_bytes=64)
                 h_words[s] = h_w
                 x_words[s] = x_w
-            in_banks[(s, piece)] = words_to_bank(pool, rows_in[s][piece // 2], 2 * (piece % 2))
+            in_banks[(s, piece)] = words_to_bank(pool, rows_in[s][piece], 0)
 
         def input_copy(s, piece):
             on_scalar = piece % 2 == 1 if s == 0 else s <= SCALAR_COPIES_UPTO
-            bank_to_words(h_words[s] if piece < 2 else x_words[s], piece % 2, in_banks[(s, piece)], on_scalar)
+            bank_to_words(h_words[s] if piece == 0 else x_words[s], 0, in_banks[(s, piece)], on_scalar)
 
         def quantise_h(s):
-            c_w = codes.tile([P, ST], U32, tag="h_codes", align_bytes=64)
-            c_s = codes.tile([P, ST], U8, tag="h_scales", align_bytes=64)
+            c_w = codes.tile([P, PR], U32, tag="h_codes", align_bytes=64)
+            c_s = codes.tile([P, PR], U8, tag="h_scales", align_bytes=64)
             quantise(c_w[:], c_s[:], h_words[s][:])
             h_codes[s] = (c_w, c_s)
 
@@ -222,7 +221,7 @@ def tile_layernormgrucell_pa_t_kernel(tc, x, h, W_r, U_r, W_c, U_c, ln_gamma, ln
             norm_banks[(unit, j)] = products(unit, j)
 
         def on_vector(unit, j, side):
-            return side == 1 and j % 2 == 1 and units.index(unit) >= len(units) - VECTOR_NORMS_LAST_UNITS
+            return side == 1 and j % 2 == 1 and units.index(unit) >= len(units) - VLAST
 
         def normalise(unit, j, vector_turn):
             if j == 0 and not vector_turn:
@@ -251,26 +250,38 @@ def tile_layernormgrucell_pa_t_kernel(tc, x, h, W_r, U_r, W_c, U_c, ln_gamma, ln
         feat_banks = {}
         summed = {}
 
-        def to_features(unit, t, side):
-            bank = tr_banks.tile([P, ST], F32, tag="bank")
-            for j in range(NJ):
-                nc.tensor.transpose(bank[:, j * P:(j + 1) * P], normal[unit][side][:, j, t * P:(t + 1) * P], ident[:])
-            feat_banks[(unit, t, side)] = bank
+        def to_features(unit, c, side):
+            bank = tr_banks.tile([P, 2, PR], F32, tag="bank")
+            for i in range(2):
+                for j in range(NJ):
+                    t = 2 * c + i
+                    nc.tensor.transpose(bank[:, i, j * P:(j + 1) * P], normal[unit][side][:, j, t * P:(t + 1) * P], ident[:])
+            feat_banks[(unit, c, side)] = bank
 
-        def first_gain(unit, t):
-            if t == 0:
-                z = sums.tile([P, NT, ST], F32, tag="z")
+        def features_a(unit, c):
+            to_features(unit, c, 0)
+
+        def features_b(unit, c):
+            to_features(unit, c, 1)
+
+        def first_gain(unit, c):
+            if c == 0:
+                z = sums.tile([P, NT, PR], F32, tag="z")
                 summed[unit] = z
             table, bias = tables[unit[1] - 1]
-            nc.scalar.activation(out=summed[unit][:, t, :], in_=feat_banks[(unit, t, 0)][:], func=ACT.Identity,
-                                 bias=bias[:, t:t + 1], scale=table[:, 2 * unit[1] - 2, t:t + 1])
+            for i in range(2):
+                t = 2 * c + i
+                nc.scalar.activation(out=summed[unit][:, t, :], in_=feat_banks[(unit, c, 0)][:, i, :], func=ACT.Identity,
+                                     bias=bias[:, t:t + 1], scale=table[:, 2 * unit[1] - 2, t:t + 1])
 
-        def second_gain(unit, t):
+        def second_gain(unit, c):
             table, bias = tables[unit[1] - 1]
             z = summed[unit]
-            nc.vector.scalar_tensor_tensor(out=z[:, t, :], in0=feat_banks[(unit, t, 1)][:],
-                                           scalar=table[:, 2 * unit[1] - 1, t:t + 1], in1=z[:, t, :],
-                                           op0=ALU.mult, op1=ALU.add)
+            for i in range(2):
+                t = 2 * c + i
+                nc.vector.scalar_tensor_tensor(out=z[:, t, :], in0=feat_banks[(unit, c, 1)][:, i, :],
+                                               scalar=table[:, 2 * unit[1] - 1, t:t + 1], in1=z[:, t, :],
+                                               op0=ALU.mult, op1=ALU.add)
 
         row_banks = {}
 
@@ -283,7 +294,8 @@ def tile_layernormgrucell_pa_t_kernel(tc, x, h, W_r, U_r, W_c, U_c, ln_gamma, ln
 
         def activate(unit, i):
             if unit[1] == 1:
-                nc.scalar.activation(out=summed[unit][:, i, :], in_=summed[unit][:, i, :], func=ACT.Sigmoid)
+                rows = summed[unit][:, :, i * P:(i + 1) * P]
+                nc.scalar.activation(out=rows, in_=rows, func=ACT.Sigmoid)
             else:
                 c_sb = outs.tile([P, D], F32, tag="c_sb")
                 nc.scalar.activation(out=c_sb[:], in_=row_banks[(unit, i)][:], func=ACT.Tanh)
@@ -296,21 +308,20 @@ def tile_layernormgrucell_pa_t_kernel(tc, x, h, W_r, U_r, W_c, U_c, ln_gamma, ln
             if stage == 2:
                 return
             if i == 0:
-                hr_w = words.tile([P, 4 * ST], BF16, tag="hr_w", align_bytes=64)
+                hr_w = words.tile([P, 4 * PR], BF16, tag="hr_w", align_bytes=64)
                 hr_words[s] = hr_w
-            for engine, lo, hi in ((nc.gpsimd, 0, G_ROWS), (nc.vector, G_ROWS, P)):
-                rows = slice(i * P + lo, i * P + hi)
-                engine.tensor_tensor(out=hr_words[s][:].rearrange("p (r t) -> p r t", t=4)[:, rows, :],
-                                     in0=summed[unit][:, :, rows].rearrange("p t r -> p r t"),
-                                     in1=h_words[s][:].rearrange("p (r t) -> p r t", t=4)[:, rows, :], op=ALU.mult)
+            rows = slice(i * P, (i + 1) * P)
+            nc.gpsimd.tensor_tensor(out=hr_words[s][:].rearrange("p (r t) -> p r t", t=4)[:, rows, :],
+                                    in0=summed[unit][:, :, rows].rearrange("p t r -> p r t"),
+                                    in1=h_words[s][:].rearrange("p (r t) -> p r t", t=4)[:, rows, :], op=ALU.mult)
 
         def quantise_hr(unit, i):
             s, stage = unit
             if stage == 2:
                 return
             if i == 0:
-                c_w = codes.tile([P, ST], U32, tag="hr_codes", bufs=5, align_bytes=64)
-                c_s = codes.tile([P, ST], U8, tag="hr_scales", bufs=5, align_bytes=64)
+                c_w = codes.tile([P, PR], U32, tag="hr_codes", bufs=10, align_bytes=64)
+                c_s = codes.tile([P, PR], U8, tag="hr_scales", bufs=10, align_bytes=64)
                 hr_codes[s] = (c_w, c_s)
             c_w, c_s = hr_codes[s]
             quantise(c_w[:, i * P:(i + 1) * P], c_s[:, i * P:(i + 1) * P], hr_words[s][:, i * 4 * P:(i + 1) * 4 * P])
@@ -319,24 +330,25 @@ def tile_layernormgrucell_pa_t_kernel(tc, x, h, W_r, U_r, W_c, U_c, ln_gamma, ln
             if 0 <= slot < slots:
                 step(units[slot // NJ], slot % NJ)
 
+        params = const.tile([P, D], BF16, name="params")
+        nc.vector.memset(params[:], 0.0)
         load_weight(0, W_r)
         load_rows(0)
         load_weight(1, U_r)
-        params = const.tile([P, D], BF16, name="params")
-        nc.vector.memset(params[:], 0.0)
+        load_rows(1)
+        load_rows(2)
+        load_rows(3)
         nc.sync.dma_start(out=params[0:4, :], in_=ln_gamma)
         nc.sync.dma_start(out=params[4:8, :], in_=ln_beta)
-        load_rows(1)
         load_weight(2, W_c)
         load_weight(3, U_c)
 
         weight_words(0, 0, mx_banks)
         weight_words(0, 1, mx_banks)
-        for piece in range(4):
-            input_transposes(0, piece, mx_banks if piece < 2 else tr_banks)
+        for piece in range(2):
+            input_transposes(0, piece, mx_banks if piece < 1 else tr_banks)
             input_copy(0, piece)
-            if piece == 1:
-                quantise_weight(0)
+        quantise_weight(0)
         quantise_h(0)
         weight_words(1, 0, tr_banks)
         weight_words(1, 1, tr_banks)
@@ -347,41 +359,40 @@ def tile_layernormgrucell_pa_t_kernel(tc, x, h, W_r, U_r, W_c, U_c, ln_gamma, ln
         run(products_for_statistics, 0)
 
         tables = []
-        for it in range(-1, slots + ACT_LAG + 1):
-            pieces = [(s, it - (first_slot[s] - INPUT_LEAD)) for s in range(1, NST)]
-            if 0 <= it - GAIN_LAG < slots:
-                to_features(units[(it - GAIN_LAG) // NJ], (it - GAIN_LAG) % NJ, 0)
+        start = 2 - INPUT_LEAD
+        for it in range(start, slots + ACT_LAG + 1):
+            pieces = [(s, it - (first_slot[s] - INPUT_LEAD)) for s in range(1, NP)]
+            moved = [(s, q // 1) for s, q in pieces if q % 1 == 0 and 0 <= q < 2 * 1]
+            run(features_a, it - GAIN_LAG)
             run(to_rows, it - ACT_LAG)
-            for s, piece in pieces:
-                if 0 <= piece < 4:
-                    input_transposes(s, piece, tr_banks)
+            for s, piece in moved:
+                input_transposes(s, piece, tr_banks)
             if 0 <= it - LATE_WEIGHTS < 4:
                 weight_words(2 + (it - LATE_WEIGHTS) // 2, (it - LATE_WEIGHTS) % 2, tr_banks)
             if it == GAIN_TABLES:
                 tables.extend(gain_tables())
-            if 0 <= it - GAIN_LAG < slots:
-                to_features(units[(it - GAIN_LAG) // NJ], (it - GAIN_LAG) % NJ, 1)
+            run(features_b, it - GAIN2_LAG)
             run(products_to_normalise, it - NORM_LAG)
             if it >= 1:
                 run(products_for_statistics, it)
             run(first_gain, it - GAIN_LAG)
             run(activate, it - ACT_LAG)
             run(normalise_on_scalar, it - NORM_LAG)
-            for s, piece in pieces:
-                if 0 <= piece < 4:
-                    input_copy(s, piece)
-                if piece == 2:
+            for s, piece in moved:
+                input_copy(s, piece)
+            for s, q in pieces:
+                if q == 2:
                     quantise_h(s)
-                if piece == 4:
+                if q == 3:
                     quantise_x(s)
             if it - LATE_WEIGHTS in (2, 4):
                 quantise_weight(1 + (it - LATE_WEIGHTS) // 2)
             run(quantise_hr, it - QUANT_LAG)
             run(multiply, it - MUL_LAG)
             run(finish_statistics, it - 1)
-            run(second_gain, it - GAIN_LAG)
+            run(second_gain, it - GAIN2_LAG)
             run(normalise_on_vector, it - NORM_LAG)
             run(statistics, it)
-            for s in range(2, NST):
-                if it == max(first_slot[s] - INPUT_LEAD - LOAD_LEAD, -1):
+            for s in range(4, NP):
+                if it == max(first_slot[s] - INPUT_LEAD - LOAD_LEAD, start):
                     load_rows(s)

@@ -27,11 +27,11 @@ GAIN2_LAG = GAIN_LAG + 0
 ACT_LAG = GAIN2_LAG + 2
 MUL_LAG = ACT_LAG + 1
 QUANT_LAG = MUL_LAG + 1
-STAGE_GAP = 7
+STAGE_GAP = 6
 INPUT_LEAD = 4
 LOAD_LEAD = 4
 LATE_WEIGHTS = 2
-GAIN_TABLES = 4
+GAIN_TABLES = 3
 SCALAR_COPIES_UPTO = 8
 VLAST = 6
 
@@ -99,10 +99,9 @@ def tile_layernormgrucell_pa_t_kernel(tc, x, h, W_r, U_r, W_c, U_c, ln_gamma, ln
 
         def load_weight(i, w):
             raw = wpool.tile([P, NT, D], BF16, tag="raw", bufs=4)
-            if i < 2:
-                nc.sync.dma_start(out=raw[:], in_=w.rearrange("(p t) k -> p t k", t=NT))
-            else:
-                nc.sync.dma_start(out=raw[:], in_=w.rearrange("(t p) k -> p t k", p=P))
+            w_v = w.rearrange("(p t) k -> p t k", t=NT) if i < 2 else w.rearrange("(t p) k -> p t k", p=P)
+            for half in range(2):
+                nc.sync.dma_start(out=raw[:, 2 * half:2 * half + 2, :], in_=w_v[:, 2 * half:2 * half + 2, :])
             w_raw[i] = raw
 
         def weight_words(i, half, pool):
@@ -150,10 +149,10 @@ def tile_layernormgrucell_pa_t_kernel(tc, x, h, W_r, U_r, W_c, U_c, ln_gamma, ln
         def quantise_x(s):
             quantise(x_codes[:, s, :], x_scales[:, s, :], x_words[s][:])
 
-        def gain_tables():
+        def gain_tables(stage):
             strided = params32[:].rearrange("p (q t) -> p t q", t=NT)
             tables = []
-            for stage in (1, 2):
+            if stage:
                 bank = tr_banks.tile([P, NT, P], F32, tag="bank")
                 for t in range(NT):
                     chunk = strided[:, t, :] if stage == 1 else params32[:, t * P:(t + 1) * P]
@@ -221,7 +220,8 @@ def tile_layernormgrucell_pa_t_kernel(tc, x, h, W_r, U_r, W_c, U_c, ln_gamma, ln
             norm_banks[(unit, j)] = products(unit, j)
 
         def on_vector(unit, j, side):
-            return side == 1 and j % 2 == 1 and units.index(unit) >= len(units) - VLAST
+            left = len(units) - units.index(unit)
+            return side == 1 and (left <= 2 or (j == 1 and left <= 8))
 
         def normalise(unit, j, vector_turn):
             if j == 0 and not vector_turn:
@@ -356,7 +356,10 @@ def tile_layernormgrucell_pa_t_kernel(tc, x, h, W_r, U_r, W_c, U_c, ln_gamma, ln
         quantise_weight(1)
         params32 = const.tile([P, D], F32, name="params32")
         nc.gpsimd.tensor_scalar(out=params32[:], in0=params[:], scalar1=1.0, scalar2=0.0, op0=ALU.mult, op1=ALU.add)
-        run(products_for_statistics, 0)
+        for it in range(2):
+            run(products_for_statistics, it)
+        for it in range(2):
+            run(statistics, it)
 
         tables = []
         start = 2 - INPUT_LEAD
@@ -369,11 +372,11 @@ def tile_layernormgrucell_pa_t_kernel(tc, x, h, W_r, U_r, W_c, U_c, ln_gamma, ln
                 input_transposes(s, piece, tr_banks)
             if 0 <= it - LATE_WEIGHTS < 4:
                 weight_words(2 + (it - LATE_WEIGHTS) // 2, (it - LATE_WEIGHTS) % 2, tr_banks)
-            if it == GAIN_TABLES:
-                tables.extend(gain_tables())
+            if it in (GAIN_TABLES, GAIN_TABLES + 1):
+                tables.extend(gain_tables(1 + it - GAIN_TABLES))
             run(features_b, it - GAIN2_LAG)
             run(products_to_normalise, it - NORM_LAG)
-            if it >= 1:
+            if it >= 2:
                 run(products_for_statistics, it)
             run(first_gain, it - GAIN_LAG)
             run(activate, it - ACT_LAG)
@@ -392,7 +395,8 @@ def tile_layernormgrucell_pa_t_kernel(tc, x, h, W_r, U_r, W_c, U_c, ln_gamma, ln
             run(finish_statistics, it - 1)
             run(second_gain, it - GAIN2_LAG)
             run(normalise_on_vector, it - NORM_LAG)
-            run(statistics, it)
+            if it >= 2:
+                run(statistics, it)
             for s in range(4, NP):
                 if it == max(first_slot[s] - INPUT_LEAD - LOAD_LEAD, start):
                     load_rows(s)

@@ -83,7 +83,7 @@ def tile_layernormgrucell_pa_t_kernel(tc, x, h, W_r, U_r, W_c, U_c, ln_gamma, ln
             return bank
 
         def bank_to_words(dst, half, bank, on_scalar):
-            dst32 = dst[:].bitcast(F32).rearrange("p (n u) -> p n u", u=2)[:, half * 2 * P:(half + 1) * 2 * P, :]
+            dst32 = dst.bitcast(F32).rearrange("p (n u) -> p n u", u=2)[:, half * 2 * P:(half + 1) * 2 * P, :]
             if on_scalar:
                 nc.scalar.copy(out=dst32, in_=bank[:].rearrange("p u n -> p n u"))
             else:
@@ -94,8 +94,8 @@ def tile_layernormgrucell_pa_t_kernel(tc, x, h, W_r, U_r, W_c, U_c, ln_gamma, ln
 
         w_raw = {}
         w_words = {}
-        w_codes = [const.tile([P, D], U32, name="w_codes%d" % i, align_bytes=64) for i in range(4)]
-        w_scales = [const.tile([P, D], U8, name="w_scales%d" % i, align_bytes=64) for i in range(4)]
+        w_codes = [const.tile([P, D], U32, name="w_codes%d" % i, align_bytes=256) for i in range(4)]
+        w_scales = [const.tile([P, D], U8, name="w_scales%d" % i, align_bytes=256) for i in range(4)]
 
         def load_weight(i, w):
             raw = wpool.tile([P, NT, D], BF16, tag="raw", bufs=4)
@@ -108,18 +108,19 @@ def tile_layernormgrucell_pa_t_kernel(tc, x, h, W_r, U_r, W_c, U_c, ln_gamma, ln
             if half == 0:
                 grouped = wpool.tile([P, 4 * D], BF16, tag="grouped", align_bytes=64)
                 w_words[i] = grouped
-            bank_to_words(w_words[i], half, words_to_bank(pool, w_raw[i], 2 * half), half == 1)
+            bank_to_words(w_words[i][:], half, words_to_bank(pool, w_raw[i], 2 * half), half == 1)
 
         def quantise_weight(i):
             quantise(w_codes[i][:], w_scales[i][:], w_words[i][:])
 
         rows_in = {}
+        in_words = {}
         h_words = {}
         x_words = {}
         in_banks = {}
         h_codes = {}
-        x_codes = const.tile([P, NP, PR], U32, name="x_codes", align_bytes=64)
-        x_scales = const.tile([P, NP, PR], U8, name="x_scales", align_bytes=64)
+        in_codes = const.tile([P, NP, 2, PR], U32, name="in_codes", align_bytes=256)
+        in_scales = const.tile([P, NP, 2, PR], U8, name="in_scales", align_bytes=256)
 
         def load_rows(s):
             h_sb = io.tile([P, NJ, D], BF16, tag="h_sb")
@@ -130,10 +131,10 @@ def tile_layernormgrucell_pa_t_kernel(tc, x, h, W_r, U_r, W_c, U_c, ln_gamma, ln
 
         def input_transposes(s, piece, pool):
             if piece == 0:
-                h_w = words.tile([P, 4 * PR], BF16, tag="h_w", bufs=10, align_bytes=64)
-                x_w = words.tile([P, 4 * PR], BF16, tag="x_w", align_bytes=64)
-                h_words[s] = h_w
-                x_words[s] = x_w
+                in_w = words.tile([P, 2, 4 * PR], BF16, tag="in_w", bufs=10, align_bytes=64)
+                in_words[s] = in_w
+                h_words[s] = in_w[:, 0, :]
+                x_words[s] = in_w[:, 1, :]
             in_banks[(s, piece)] = words_to_bank(pool, rows_in[s][piece], 0)
 
         def input_copy(s, piece):
@@ -141,13 +142,12 @@ def tile_layernormgrucell_pa_t_kernel(tc, x, h, W_r, U_r, W_c, U_c, ln_gamma, ln
             bank_to_words(h_words[s] if piece == 0 else x_words[s], 0, in_banks[(s, piece)], on_scalar)
 
         def quantise_h(s):
-            c_w = codes.tile([P, PR], U32, tag="h_codes", align_bytes=64)
-            c_s = codes.tile([P, PR], U8, tag="h_scales", align_bytes=64)
-            quantise(c_w[:], c_s[:], h_words[s][:])
-            h_codes[s] = (c_w, c_s)
+            pass
 
         def quantise_x(s):
-            quantise(x_codes[:, s, :], x_scales[:, s, :], x_words[s][:])
+            quantise(in_codes[:, s].rearrange("p i n -> p (i n)"), in_scales[:, s].rearrange("p i n -> p (i n)"),
+                     in_words[s][:].rearrange("p i n -> p (i n)"))
+            h_codes[s] = (in_codes[:, s, 0, :], in_scales[:, s, 0, :])
 
         def gain_tables(stage):
             strided = params32[:].rearrange("p (q t) -> p t q", t=NT)
@@ -176,7 +176,7 @@ def tile_layernormgrucell_pa_t_kernel(tc, x, h, W_r, U_r, W_c, U_c, ln_gamma, ln
             a_w, a_s = h_codes[s] if stage == 1 else hr_codes[s]
             pair = []
             for lhs_w, lhs_s, i in ((a_w[:, cols], a_s[:, cols], 2 * stage - 2),
-                                    (x_codes[:, s, cols], x_scales[:, s, cols], 2 * stage - 1)):
+                                    (in_codes[:, s, 1, cols], in_scales[:, s, 1, cols], 2 * stage - 1)):
                 bank = mx_banks.tile([P, D], F32, tag="bank")
                 nc.tensor.matmul_mx(out=bank[:], lhsT=lhs_w.bitcast(FP8X4), lhsT_scale=lhs_s,
                                     rhs=w_codes[i][:].bitcast(FP8X4), rhs_scale=w_scales[i][:], start=True, stop=True)
@@ -313,15 +313,15 @@ def tile_layernormgrucell_pa_t_kernel(tc, x, h, W_r, U_r, W_c, U_c, ln_gamma, ln
             rows = slice(i * P, (i + 1) * P)
             nc.gpsimd.tensor_tensor(out=hr_words[s][:].rearrange("p (r t) -> p r t", t=4)[:, rows, :],
                                     in0=summed[unit][:, :, rows].rearrange("p t r -> p r t"),
-                                    in1=h_words[s][:].rearrange("p (r t) -> p r t", t=4)[:, rows, :], op=ALU.mult)
+                                    in1=h_words[s].rearrange("p (r t) -> p r t", t=4)[:, rows, :], op=ALU.mult)
 
         def quantise_hr(unit, i):
             s, stage = unit
             if stage == 2:
                 return
             if i == 0:
-                c_w = codes.tile([P, PR], U32, tag="hr_codes", bufs=10, align_bytes=64)
-                c_s = codes.tile([P, PR], U8, tag="hr_scales", bufs=10, align_bytes=64)
+                c_w = codes.tile([P, PR], U32, tag="hr_codes", bufs=10, align_bytes=256)
+                c_s = codes.tile([P, PR], U8, tag="hr_scales", bufs=10, align_bytes=256)
                 hr_codes[s] = (c_w, c_s)
             c_w, c_s = hr_codes[s]
             quantise(c_w[:, i * P:(i + 1) * P], c_s[:, i * P:(i + 1) * P], hr_words[s][:, i * 4 * P:(i + 1) * 4 * P])

@@ -74,6 +74,15 @@ def tile_layernormgrucell_pa_t_kernel(tc, x, h, W_r, U_r, W_c, U_c, ln_gamma, ln
         nc.vector.memset(warm[:], 0.0)
         nc.scalar.activation(out=warm[:], in_=warm[:], func=ACT.Sigmoid)
 
+        zeros = const.tile([P, D], BF16, name="zeros")
+        nc.vector.memset(zeros[:], 0.0)
+
+        def keep_warm(count):
+            if count:
+                bank = mx_banks.tile([P, D], F32, tag="bank")
+                for repeat in range(count):
+                    nc.tensor.matmul(bank[:], lhsT=zeros[:, :P], rhs=zeros[:], start=True, stop=True)
+
         def words_to_bank(pool, src, first):
             bank = pool.tile([P, 2, 2 * P], F32, tag="bank")
             for i in range(2):
@@ -343,15 +352,19 @@ def tile_layernormgrucell_pa_t_kernel(tc, x, h, W_r, U_r, W_c, U_c, ln_gamma, ln
         load_weight(2, W_c)
         load_weight(3, U_c)
 
-        weight_words(0, 0, mx_banks)
-        weight_words(0, 1, mx_banks)
+        keep_warm(5)
+        weight_words(0, 0, tr_banks)
+        weight_words(0, 1, tr_banks)
+        keep_warm(2)
         for piece in range(2):
-            input_transposes(0, piece, mx_banks if piece < 1 else tr_banks)
+            input_transposes(0, piece, tr_banks)
             input_copy(0, piece)
         quantise_weight(0)
         quantise_h(0)
+        keep_warm(2)
         weight_words(1, 0, tr_banks)
         weight_words(1, 1, tr_banks)
+        keep_warm(1)
         quantise_x(0)
         quantise_weight(1)
         params32 = const.tile([P, D], F32, name="params32")

@@ -320,7 +320,7 @@ def tile_layernormgrucell_pa_t_kernel(tc, x, h, W_r, U_r, W_c, U_c, ln_gamma, ln
                 hr_w = words.tile([P, 4 * PR], BF16, tag="hr_w", align_bytes=64)
                 hr_words[s] = hr_w
             rows = slice(i * P, (i + 1) * P)
-            nc.gpsimd.tensor_tensor(out=hr_words[s][:].rearrange("p (r t) -> p r t", t=4)[:, rows, :],
+            (nc.vector if s < 6 and i == 1 else nc.gpsimd).tensor_tensor(out=hr_words[s][:].rearrange("p (r t) -> p r t", t=4)[:, rows, :],
                                     in0=summed[unit][:, :, rows].rearrange("p t r -> p r t"),
                                     in1=h_words[s].rearrange("p (r t) -> p r t", t=4)[:, rows, :], op=ALU.mult)
 

@@ -31,7 +31,7 @@ STAGE_GAP = 6
 INPUT_LEAD = 4
 LOAD_LEAD = 4
 LATE_WEIGHTS = 2
-GAIN_TABLES = 3
+GAIN_TABLES = 0
 SCALAR_COPIES_UPTO = 8
 VLAST = 6
 
@@ -403,10 +403,10 @@ def tile_layernormgrucell_pa_t_kernel(tc, x, h, W_r, U_r, W_c, U_c, ln_gamma, ln
                     quantise_x(s)
             if it - LATE_WEIGHTS in (2, 4):
                 quantise_weight(1 + (it - LATE_WEIGHTS) // 2)
+            run(second_gain, it - GAIN2_LAG)
             run(quantise_hr, it - QUANT_LAG)
             run(multiply, it - MUL_LAG)
             run(finish_statistics, it - 1)
-            run(second_gain, it - GAIN2_LAG)
             run(normalise_on_vector, it - NORM_LAG)
             if it >= 2:
                 run(statistics, it)

from contextlib import ExitStack

import concourse.mybir as mybir
from concourse.masks import make_identity

F32 = mybir.dt.float32
BF16 = mybir.dt.bfloat16
U32 = mybir.dt.uint32
U8 = mybir.dt.uint8
FP8X4 = mybir.dt.float8_e4m3fn_x4
ACT = mybir.ActivationFunctionType
ALU = mybir.AluOpType

P = 128
ROWS = 4096
D = 512
PR = 256
NP = ROWS // PR
NJ = PR // P
NT = D // P
EPS = 1e-5
FLOPS = 4 * 2 * ROWS * D * D
CHAIN = 2
NORM_LAG = 4
GAIN_LAG = NORM_LAG + 3
GAIN2_LAG = GAIN_LAG + 0
ACT_LAG = GAIN2_LAG + 2
MUL_LAG = ACT_LAG + 1
QUANT_LAG = MUL_LAG + 1
STAGE_GAP = 6
INPUT_LEAD = 4
LOAD_LEAD = 4
LATE_WEIGHTS = 2
GAIN_TABLES = 0
SCALAR_COPIES_UPTO = 8
VLAST = 6


def unit_order():
    order = [(s, 1) for s in range(STAGE_GAP)]
    for s in range(NP - STAGE_GAP):
        order += [(s, 2), (s + STAGE_GAP, 1)]
    return order + [(s, 2) for s in range(NP - STAGE_GAP, NP)]


def tile_layernormgrucell_pa_t_kernel(tc, x, h, W_r, U_r, W_c, U_c, ln_gamma, ln_beta, out):
    nc = tc.nc
    x_v = x.rearrange("(s j p) k -> p s j k", s=NP, j=NJ)
    h_v = h.rearrange("(s j p) k -> p s j k", s=NP, j=NJ)
    out_v = out.rearrange("(s j p) f -> p s j f", s=NP, j=NJ)
    units = unit_order()
    slots = NJ * len(units)
    first_slot = {s: NJ * units.index((s, 1)) for s in range(NP)}

    with ExitStack() as ctx:
        ctx.enter_context(tc.manual_schedule())
        const = ctx.enter_context(tc.tile_pool(name="const", bufs=1))
        wpool = ctx.enter_context(tc.tile_pool(name="wpool", bufs=2))
        io = ctx.enter_context(tc.tile_pool(name="io", bufs=4))
        words = ctx.enter_context(tc.tile_pool(name="words", bufs=3))
        codes = ctx.enter_context(tc.tile_pool(name="codes", bufs=4))
        normed = ctx.enter_context(tc.tile_pool(name="normed", bufs=4))
        sums = ctx.enter_context(tc.tile_pool(name="sums", bufs=6))
        outs = ctx.enter_context(tc.tile_pool(name="outs", bufs=4))
        small = ctx.enter_context(tc.tile_pool(name="small", bufs=8))
        mx_banks = ctx.enter_context(tc.psum_pool(name="mx_banks", bufs=4))
        tr_banks = ctx.enter_context(tc.psum_pool(name="tr_banks", bufs=4))

        ident = const.tile([P, P], F32, name="ident")
        make_identity(nc, ident[:])
        minus_half = const.tile([P, 2 * CHAIN], F32, name="minus_half")
        nc.gpsimd.memset(minus_half[:], -0.5)
        warm = const.tile([P, 1], F32, name="warm")
        nc.vector.memset(warm[:], 0.0)
        nc.scalar.activation(out=warm[:], in_=warm[:], func=ACT.Sigmoid)

        zeros = const.tile([P, D], BF16, name="zeros")
        nc.vector.memset(zeros[:], 0.0)

        def keep_warm(count):
            if count:
                bank = mx_banks.tile([P, D], F32, tag="bank")
                for repeat in range(count):
                    nc.tensor.matmul(bank[:], lhsT=zeros[:, :P], rhs=zeros[:], start=True, stop=True)

        def words_to_bank(pool, src, first):
            bank = pool.tile([P, 2, 2 * P], F32, tag="bank")
            for i in range(2):
                src32 = src[:, first + i, :].bitcast(F32).rearrange("p (w u) -> p u w", u=2)
                for u in range(2):
                    nc.tensor.transpose(bank[:, u, i * P:(i + 1) * P], src32[:, u, :], ident[:])
            return bank

        def bank_to_words(dst, half, bank, on_scalar):
            dst32 = dst.bitcast(F32).rearrange("p (n u) -> p n u", u=2)[:, half * 2 * P:(half + 1) * 2 * P, :]
            if on_scalar:
                nc.scalar.copy(out=dst32, in_=bank[:].rearrange("p u n -> p n u"))
            else:
                nc.vector.tensor_copy(out=dst32, in_=bank[:].rearrange("p u n -> p n u"))

        def quantise(code_words, scales, src):
            nc.vector.quantize_mx(out=code_words.bitcast(FP8X4), scales=scales, in_=src)

        w_raw = {}
        w_words = {}
        w_codes = [const.tile([P, D], U32, name="w_codes%d" % i, align_bytes=256) for i in range(4)]
        w_scales = [const.tile([P, D], U8, name="w_scales%d" % i, align_bytes=256) for i in range(4)]

        def load_weight(i, w):
            raw = wpool.tile([P, NT, D], BF16, tag="raw", bufs=4)
            w_v = w.rearrange("(p t) k -> p t k", t=NT) if i < 2 else w.rearrange("(t p) k -> p t k", p=P)
            for half in range(2):
                nc.sync.dma_start(out=raw[:, 2 * half:2 * half + 2, :], in_=w_v[:, 2 * half:2 * half + 2, :])
            w_raw[i] = raw

        def weight_words(i, half, pool):
            if half == 0:
                grouped = wpool.tile([P, 4 * D], BF16, tag="grouped", align_bytes=64)
                w_words[i] = grouped
            bank_to_words(w_words[i][:], half, words_to_bank(pool, w_raw[i], 2 * half), half == 1)

        def quantise_weight(i):
            quantise(w_codes[i][:], w_scales[i][:], w_words[i][:])

        rows_in = {}
        in_words = {}
        h_words = {}
        x_words = {}
        in_banks = {}
        h_codes = {}
        in_codes = const.tile([P, NP, 2, PR], U32, name="in_codes", align_bytes=256)
        in_scales = const.tile([P, NP, 2, PR], U8, name="in_scales", align_bytes=256)

        def load_rows(s):
            h_sb = io.tile([P, NJ, D], BF16, tag="h_sb")
            nc.sync.dma_start(out=h_sb[:], in_=h_v[:, s])
            x_sb = io.tile([P, NJ, D], BF16, tag="x_sb")
            nc.sync.dma_start(out=x_sb[:], in_=x_v[:, s])
            rows_in[s] = (h_sb, x_sb)

        def input_transposes(s, piece, pool):
            if piece == 0:
                in_w = words.tile([P, 2, 4 * PR], BF16, tag="in_w", bufs=10, align_bytes=64)
                in_words[s] = in_w
                h_words[s] = in_w[:, 0, :]
                x_words[s] = in_w[:, 1, :]
            in_banks[(s, piece)] = words_to_bank(pool, rows_in[s][piece], 0)

        def input_copy(s, piece):
            on_scalar = piece % 2 == 1 if s == 0 else s <= SCALAR_COPIES_UPTO
            bank_to_words(h_words[s] if piece == 0 else x_words[s], 0, in_banks[(s, piece)], on_scalar)

        def quantise_h(s):
            pass

        def quantise_x(s):
            quantise(in_codes[:, s].rearrange("p i n -> p (i n)"), in_scales[:, s].rearrange("p i n -> p (i n)"),
                     in_words[s][:].rearrange("p i n -> p (i n)"))
            h_codes[s] = (in_codes[:, s, 0, :], in_scales[:, s, 0, :])

        def gain_tables(stage):
            strided = params32[:].rearrange("p (q t) -> p t q", t=NT)
            tables = []
            if stage:
                bank = tr_banks.tile([P, NT, P], F32, tag="bank")
                for t in range(NT):
                    chunk = strided[:, t, :] if stage == 1 else params32[:, t * P:(t + 1) * P]
                    nc.tensor.transpose(bank[:, t, :], chunk, ident[:])
                table = const.tile([P, 8, NT], F32, name="table%d" % stage)
                nc.vector.tensor_copy(out=table[:], in_=bank[:, :, 0:8].rearrange("p c i -> p i c"))
                bias = const.tile([P, NT], F32, name="bias%d" % stage)
                nc.vector.tensor_tensor(out=bias[:], in0=table[:, 2 + 2 * stage, :], in1=table[:, 3 + 2 * stage, :],
                                        op=ALU.add)
                tables.append((table, bias))
            return tables

        hr_codes = {}
        stat_banks = {}
        stat_parts = {}
        moments = {}

        def products(unit, j):
            s, stage = unit
            cols = slice(j * P, (j + 1) * P)
            a_w, a_s = h_codes[s] if stage == 1 else hr_codes[s]
            pair = []
            for lhs_w, lhs_s, i in ((a_w[:, cols], a_s[:, cols], 2 * stage - 2),
                                    (in_codes[:, s, 1, cols], in_scales[:, s, 1, cols], 2 * stage - 1)):
                bank = mx_banks.tile([P, D], F32, tag="bank")
                nc.tensor.matmul_mx(out=bank[:], lhsT=lhs_w.bitcast(FP8X4), lhsT_scale=lhs_s,
                                    rhs=w_codes[i][:].bitcast(FP8X4), rhs_scale=w_scales[i][:], start=True, stop=True)
                pair.append(bank)
            return pair

        def products_for_statistics(unit, j):
            stat_banks[(unit, j)] = products(unit, j)

        def statistics(unit, j):
            parts = small.tile([P, 2, 6], F32, tag="parts")
            for side in range(2):
                nc.vector.bn_stats(out=parts[:, side, :], in_=stat_banks[(unit, j)][side][:])
            stat_parts[(unit, j)] = parts

        def finish_statistics(unit, j):
            k = 2 * (j % CHAIN)
            if k == 0:
                mean_var = small.tile([P, 2 * CHAIN, 2], F32, tag="mean_var")
                moments[(unit, j // CHAIN)] = [mean_var]
            mean_var = moments[(unit, j // CHAIN)][0]
            for side in range(2):
                nc.vector.bn_aggr(out=mean_var[:, k + side, :], in_=stat_parts[(unit, j)][:, side, :])
            if j % CHAIN == CHAIN - 1:
                var_eps = small.tile([P, 2 * CHAIN], F32, tag="var_eps")
                nc.gpsimd.tensor_scalar(out=var_eps[:], in0=mean_var[:, :, 1], scalar1=1.0, scalar2=EPS,
                                        op0=ALU.mult, op1=ALU.add)
                rstd = small.tile([P, 2 * CHAIN], F32, tag="rstd")
                nc.gpsimd.tensor_tensor(out=rstd[:], in0=var_eps[:], in1=minus_half[:], op=ALU.pow)
                mean_rstd = small.tile([P, 2 * CHAIN], F32, tag="mean_rstd")
                nc.gpsimd.tensor_tensor(out=mean_rstd[:], in0=mean_var[:, :, 0], in1=rstd[:], op=ALU.mult)
                shift = small.tile([P, 2 * CHAIN], F32, tag="shift")
                nc.gpsimd.tensor_scalar(out=shift[:], in0=mean_rstd[:], scalar1=-1.0, scalar2=0.0,
                                        op0=ALU.mult, op1=ALU.add)
                moments[(unit, j // CHAIN)] += [rstd, shift]

        norm_banks = {}
        normal = {}

        def products_to_normalise(unit, j):
            norm_banks[(unit, j)] = products(unit, j)

        def on_vector(unit, j, side):
            left = len(units) - units.index(unit)
            return side == 1 and (left <= 2 or (j == 1 and left <= 8))

        def normalise(unit, j, vector_turn):
            if j == 0 and not vector_turn:
                n_a = normed.tile([P, NJ, D], F32, tag="n_a")
                n_b = normed.tile([P, NJ, D], F32, tag="n_b")
                normal[unit] = (n_a, n_b)
            mean_var, rstd, shift = moments[(unit, j // CHAIN)]
            for side in range(2):
                k = 2 * (j % CHAIN) + side
                if on_vector(unit, j, side) != vector_turn:
                    continue
                if vector_turn:
                    nc.vector.tensor_scalar(out=normal[unit][side][:, j, :], in0=norm_banks[(unit, j)][side][:],
                                            scalar1=mean_var[:, k, 0:1], scalar2=rstd[:, k:k + 1],
                                            op0=ALU.subtract, op1=ALU.mult)
                else:
                    nc.scalar.activation(out=normal[unit][side][:, j, :], in_=norm_banks[(unit, j)][side][:],
                                         func=ACT.Identity, bias=shift[:, k:k + 1], scale=rstd[:, k:k + 1])

        def normalise_on_scalar(unit, j):
            normalise(unit, j, False)

        def normalise_on_vector(unit, j):
            normalise(unit, j, True)

        feat_banks = {}
        summed = {}

        def to_features(unit, c, side):
            bank = tr_banks.tile([P, 2, PR], F32, tag="bank")
            for i in range(2):
                for j in range(NJ):
                    t = 2 * c + i
                    nc.tensor.transpose(bank[:, i, j * P:(j + 1) * P], normal[unit][side][:, j, t * P:(t + 1) * P], ident[:])
            feat_banks[(unit, c, side)] = bank

        def features_a(unit, c):
            to_features(unit, c, 0)

        def features_b(unit, c):
            to_features(unit, c, 1)

        def first_gain(unit, c):
            if c == 0:
                z = sums.tile([P, NT, PR], F32, tag="z")
                summed[unit] = z
            table, bias = tables[unit[1] - 1]
            for i in range(2):
                t = 2 * c + i
                nc.scalar.activation(out=summed[unit][:, t, :], in_=feat_banks[(unit, c, 0)][:, i, :], func=ACT.Identity,
                                     bias=bias[:, t:t + 1], scale=table[:, 2 * unit[1] - 2, t:t + 1])

        def second_gain(unit, c):
            table, bias = tables[unit[1] - 1]
            z = summed[unit]
            for i in range(2):
                t = 2 * c + i
                nc.vector.scalar_tensor_tensor(out=z[:, t, :], in0=feat_banks[(unit, c, 1)][:, i, :],
                                               scalar=table[:, 2 * unit[1] - 1, t:t + 1], in1=z[:, t, :],
                                               op0=ALU.mult, op1=ALU.add)

        row_banks = {}

        def to_rows(unit, i):
            if unit[1] == 2:
                bank = tr_banks.tile([P, D], F32, tag="bank")
                for t in range(NT):
                    nc.tensor.transpose(bank[:, t * P:(t + 1) * P], summed[unit][:, t, i * P:(i + 1) * P], ident[:])
                row_banks[(unit, i)] = bank

        def activate(unit, i):
            if unit[1] == 1:
                rows = summed[unit][:, :, i * P:(i + 1) * P]
                nc.scalar.activation(out=rows, in_=rows, func=ACT.Sigmoid)
            else:
                c_sb = outs.tile([P, D], F32, tag="c_sb")
                nc.scalar.activation(out=c_sb[:], in_=row_banks[(unit, i)][:], func=ACT.Tanh)
                nc.sync.dma_start(out=out_v[:, unit[0], i, :], in_=c_sb[:])

        hr_words = {}

        def multiply(unit, i):
            s, stage = unit
            if stage == 2:
                return
            if i == 0:
                hr_w = words.tile([P, 4 * PR], BF16, tag="hr_w", align_bytes=64)
                hr_words[s] = hr_w
            rows = slice(i * P, (i + 1) * P)
            (nc.vector if s < 6 and i == 1 else nc.gpsimd).tensor_tensor(out=hr_words[s][:].rearrange("p (r t) -> p r t", t=4)[:, rows, :],
                                    in0=summed[unit][:, :, rows].rearrange("p t r -> p r t"),
                                    in1=h_words[s].rearrange("p (r t) -> p r t", t=4)[:, rows, :], op=ALU.mult)

        def quantise_hr(unit, i):
            s, stage = unit
            if stage == 2:
                return
            if i == 0:
                c_w = codes.tile([P, PR], U32, tag="hr_codes", bufs=10, align_bytes=256)
                c_s = codes.tile([P, PR], U8, tag="hr_scales", bufs=10, align_bytes=256)
                hr_codes[s] = (c_w, c_s)
            c_w, c_s = hr_codes[s]
            quantise(c_w[:, i * P:(i + 1) * P], c_s[:, i * P:(i + 1) * P], hr_words[s][:, i * 4 * P:(i + 1) * 4 * P])

        def run(step, slot):
            if 0 <= slot < slots:
                step(units[slot // NJ], slot % NJ)

        params = const.tile([P, D], BF16, name="params")
        nc.vector.memset(params[:], 0.0)
        load_weight(0, W_r)
        load_rows(0)
        load_weight(1, U_r)
        load_rows(1)
        load_rows(2)
        load_rows(3)
        nc.sync.dma_start(out=params[0:4, :], in_=ln_gamma)
        nc.sync.dma_start(out=params[4:8, :], in_=ln_beta)
        load_weight(2, W_c)
        load_weight(3, U_c)

        keep_warm(5)
        weight_words(0, 0, tr_banks)
        weight_words(0, 1, tr_banks)
        keep_warm(2)
        for piece in range(2):
            input_transposes(0, piece, tr_banks)
            input_copy(0, piece)
        quantise_weight(0)
        quantise_h(0)
        keep_warm(2)
        weight_words(1, 0, tr_banks)
        weight_words(1, 1, tr_banks)
        keep_warm(1)
        quantise_x(0)
        quantise_weight(1)
        params32 = const.tile([P, D], F32, name="params32")
        nc.gpsimd.tensor_scalar(out=params32[:], in0=params[:], scalar1=1.0, scalar2=0.0, op0=ALU.mult, op1=ALU.add)
        for it in range(2):
            run(products_for_statistics, it)
        for it in range(2):
            run(statistics, it)

        tables = []
        start = 2 - INPUT_LEAD
        for it in range(start, slots + ACT_LAG + 1):
            pieces = [(s, it - (first_slot[s] - INPUT_LEAD)) for s in range(1, NP)]
            moved = [(s, q // 1) for s, q in pieces if q % 1 == 0 and 0 <= q < 2 * 1]
            run(features_a, it - GAIN_LAG)
            run(to_rows, it - ACT_LAG)
            for s, piece in moved:
                input_transposes(s, piece, tr_banks)
            if 0 <= it - LATE_WEIGHTS < 4:
                weight_words(2 + (it - LATE_WEIGHTS) // 2, (it - LATE_WEIGHTS) % 2, tr_banks)
            if it in (GAIN_TABLES, GAIN_TABLES + 1):
                tables.extend(gain_tables(1 + it - GAIN_TABLES))
            run(features_b, it - GAIN2_LAG)
            run(products_to_normalise, it - NORM_LAG)
            if it >= 2:
                run(products_for_statistics, it)
            run(first_gain, it - GAIN_LAG)
            run(activate, it - ACT_LAG)
            run(normalise_on_scalar, it - NORM_LAG)
            for s, piece in moved:
                input_copy(s, piece)
            for s, q in pieces:
                if q == 2:
                    quantise_h(s)
                if q == 3:
                    quantise_x(s)
            if it - LATE_WEIGHTS in (2, 4):
                quantise_weight(1 + (it - LATE_WEIGHTS) // 2)
            run(second_gain, it - GAIN2_LAG)
            run(quantise_hr, it - QUANT_LAG)
            run(multiply, it - MUL_LAG)
            run(finish_statistics, it - 1)
            run(normalise_on_vector, it - NORM_LAG)
            if it >= 2:
                run(statistics, it)
            for s in range(4, NP):
                if it == max(first_slot[s] - INPUT_LEAD - LOAD_LEAD, start):
                    load_rows(s)
